import numpy as np
import ml_dtypes


def mxq(x, axis, fmt="e4m3"):
    dtype, down = {"e4m3": (ml_dtypes.float8_e4m3fn, 7), "e5m2": (ml_dtypes.float8_e5m2, 14)}[fmt]
    v = np.moveaxis(np.asarray(x, np.float32).astype(ml_dtypes.bfloat16).astype(np.float64), axis, -1)
    blocks = v.reshape(v.shape[:-1] + (-1, 32))
    amax = np.abs(blocks).max(-1, keepdims=True)
    byte = np.maximum(np.where(amax > 0, np.frexp(amax)[1] - 1 + 127, 0) - down, 1)
    scale = np.exp2(byte - 127.0)
    codes = (blocks / scale).astype(np.float32).astype(dtype).astype(np.float64)
    return np.moveaxis((codes * scale).reshape(v.shape), -1, axis)


WIDE = False


def mx_kscale(k):
    if not WIDE:
        return np.ones(k)
    levels = np.array([10, -10, 5, -5, 0])
    if k % 512:
        return np.exp2(np.random.permutation(np.resize(levels, k // 32))).repeat(32)
    a = np.empty((k // 512, 16))
    for p in range(k // 512):
        a[p, :8] = np.random.permutation(np.resize(levels, 8))
        for g in range(8):
            far = levels[np.abs(levels - a[p, g]) >= 10]
            a[p, g + 8] = far[np.random.randint(len(far))]
    return np.exp2(a.ravel()).repeat(32)


BF16 = ml_dtypes.bfloat16


def bf(x):
    return np.asarray(x, np.float32).astype(BF16)


def f64(x):
    return np.asarray(x).astype(np.float64)


B, NC, APC, D = 512, 8, 512, 512
H = 2 * D
LN_EPS = 1e-5


def setup_inputs():
    s = mx_kscale(APC)
    t = np.exp2(np.round(np.log2(mx_kscale(H)) / 2))
    return {"tri": bf(np.random.standard_normal((B, APC * NC)) * np.repeat(s, NC)),
            "W1": bf(np.random.standard_normal((NC, APC, H)) / np.sqrt(APC) / s[None, :, None] * t),
            "b1": bf(np.random.standard_normal((NC, H)) * 0.1 * t),
            "W2": bf(np.random.standard_normal((NC, H, D)) / np.sqrt(H) / (t * t)[None, :, None]),
            "b2": bf(np.random.standard_normal((NC, D)) * 0.1),
            "gamma": bf(1.0 + 0.1 * np.random.standard_normal((NC, D))),
            "beta": bf(np.random.standard_normal((NC, D)) * 0.1)}


def reference(tri, W1, b1, W2, b2, gamma, beta):
    tri, W1, b1, W2, b2, gamma, beta = f64(tri), f64(W1), f64(b1), f64(W2), f64(b2), f64(gamma), f64(beta)
    b, n_anchors = tri.shape
    n_comp, apc, _ = W1.shape
    d = W2.shape[2]
    x = np.transpose(tri.reshape(b, apc, n_comp), (2, 0, 1))
    h = f64(bf(mxq(x, 2, "e4m3") @ mxq(W1, 1, "e4m3"))) + b1[:, None, :]
    h = np.square(np.maximum(h, 0.0))
    y = (mxq(h, 2, "e4m3") @ mxq(W2, 1, "e4m3")) + b2[:, None, :]
    mu = np.mean(y, axis=-1, keepdims=True)
    var = np.mean(np.square(y - mu), axis=-1, keepdims=True)
    y = (y - mu) * (1.0 / np.sqrt(var + LN_EPS))
    y = y * gamma[:, None, :] + beta[:, None, :]
    return np.transpose(y, (1, 0, 2)).reshape(b, n_comp * d)

from contextlib import ExitStack

import concourse.mybir as mybir
from concourse.masks import make_identity

B, NC, APC, D = 512, 8, 512, 512
H = 2 * D
LN_EPS = 1e-5
FLOPS = 2 * NC * B * (APC * H + H * D)

F32 = mybir.dt.float32
BF16 = mybir.dt.bfloat16
U32 = mybir.dt.uint32
U8 = mybir.dt.uint8
FP8X4 = mybir.dt.float8_e4m3fn_x4
ACT = mybir.ActivationFunctionType
ALU = mybir.AluOpType

P = 128
BT = B // P
G = H // 512
BP = B // 2
BANK1 = BF16
PE_CHUNKS = [14,18,22,26,30]
X_HEAD = 3


def tile_patchwork_kernel(tc, tri, W1, b1, W2, b2, gamma, beta, out):
    nc = tc.nc
    with ExitStack() as ctx:
        const = ctx.enter_context(tc.tile_pool(name="const", bufs=1))
        raw = ctx.enter_context(tc.tile_pool(name="raw", bufs=2))
        wgp = ctx.enter_context(tc.tile_pool(name="wgp", bufs=3))
        codes = ctx.enter_context(tc.tile_pool(name="codes", bufs=2))
        xp = ctx.enter_context(tc.tile_pool(name="xp", bufs=3))
        hp = ctx.enter_context(tc.tile_pool(name="hp", bufs=2))
        ep = ctx.enter_context(tc.tile_pool(name="ep", bufs=4))
        st = ctx.enter_context(tc.tile_pool(name="st", bufs=4))
        psum = ctx.enter_context(tc.psum_pool(name="psum", bufs=7))
        psc = ctx.enter_context(tc.psum_pool(name="psc", bufs=1))
        ctx.enter_context(tc.manual_schedule())

        w1raw, w2raw, w1c, w1s, w2c, w2s = {}, {}, {}, {}, {}, {}
        wg, xg, xc, xs, tp, pil = {}, {}, {}, {}, {}, {}
        bank1, rr, hg, hc, hs, ybank = {}, {}, {}, {}, {}, {}
        yy, cg, negmu, rstd, gb, b2t, b2ps = {}, {}, {}, {}, {}, {}, {}
        ysum, ssq, std = {}, {}, {}
        state = {"chunk": 0}

        def ok(k):
            return 0 <= k < NC

        def load_w1(k):
            if ok(k):
                for g in range(G):
                    w1raw[k, g] = raw.tile([P, 4, 512], BF16, tag="w1raw", name="w1raw", bufs=4)
                    nc.sync.dma_start(out=w1raw[k, g][:],
                                      in_=W1[k][:, g * 512:(g + 1) * 512].rearrange("(p j) h -> p j h", j=4))

        def load_w2(k):
            if ok(k):
                w2raw[k] = raw.tile([P, G, 4, D], BF16, tag="w2raw", name="w2raw")
                nc.sync.dma_start(out=w2raw[k][:], in_=W2[k].rearrange("(g p j) d -> p g j d", g=G, j=4))

        def w_source(c):
            k, part = divmod(c, 4)
            g = part % 2
            if part < 2:
                return w1raw[k, g][:].rearrange("p j (m t) -> p t m j", t=4)
            return w2raw[k][:, g].rearrange("p j (q d) -> p q d j", q=4)

        def w_interleave_pe(c):
            if c in PE_CHUNKS:
                src = w_source(c)
                for half in range(2):
                    pil[c, half] = psum.tile([P, 2, P, 4], BF16, tag="bank", name="pil")
                    for u in range(2):
                        nc.tensor.matmul(out=pil[c, half][:, u], lhsT=ident[:], rhs=src[:, 2 * half + u],
                                         start=True, stop=True)

        def w_interleave(c):
            k, part = divmod(c, 4)
            wg[c] = wgp.tile([P, 2048], BF16, tag="wg", name="wg", align_bytes=64)
            if c in PE_CHUNKS:
                for half in range(2):
                    nc.scalar.copy(out=wg[c][:, half * 1024:(half + 1) * 1024],
                                   in_=pil[c, half][:].rearrange("p u m j -> p (u m j)"))
            else:
                if part < 2:
                    nc.vector.tensor_copy(out=wg[c][:].rearrange("p (q m j) -> p q m j", q=4, j=4), in_=w_source(c))
                else:
                    nc.vector.tensor_copy(out=wg[c][:].rearrange("p (c i j) -> p c j i", i=4, j=4),
                                          in_=w2raw[k][:, part % 2].rearrange("p j (c i) -> p c j i", i=4))
            if part == 1:
                load_w1(k + 2)
            if part == 3:
                load_w2(k + 2)

        def w_quantize(c):
            k, part = divmod(c, 4)
            g = part % 2
            if part == 0:
                w1c[k] = codes.tile([P, G, 512], U32, tag="w1c", name="w1c", align_bytes=64)
                w1s[k] = codes.tile([P, G, 512], U8, tag="w1s", name="w1s", align_bytes=64)
            if part == 2:
                w2c[k] = codes.tile([P, G, D], U32, tag="w2c", name="w2c", align_bytes=64)
                w2s[k] = codes.tile([P, G, D], U8, tag="w2s", name="w2s", align_bytes=64)
            wc, ws = (w1c[k], w1s[k]) if part < 2 else (w2c[k], w2s[k])
            nc.vector.quantize_mx(out=wc[:, g, :].bitcast(FP8X4), scales=ws[:, g, :], in_=wg[c][:])

        def fill():
            c = state["chunk"]
            if c <= 4 * NC:
                w_quantize(c - 1)
            if c < 4 * NC:
                w_interleave(c)
            w_interleave_pe(c + 1)
            state["chunk"] = c + 1

        def x_transposes(k, bt):
            if not ok(k):
                return
            half, bl = divmod(bt, 2)
            if bl == 0:
                tp[k, half] = psum.tile([P, 4, BP], BF16, tag="bank", name="tp")
            for t in range(4):
                nc.tensor.transpose(tp[k, half][:, t, bl * P:(bl + 1) * P],
                                    tri_sb[bt][:, 8 * t + k:APC * NC:32], ident[:])

        def x_copy(k, half, engine):
            if not ok(k):
                return
            xg[k, half] = xp.tile([P, 4 * BP], BF16, tag="xg", name="xg", align_bytes=64)
            dst = xg[k, half][:].rearrange("p (b t) -> p b t", t=4)
            if engine == "S":
                nc.scalar.copy(out=dst, in_=tp[k, half][:].rearrange("p t b -> p b t"))
            else:
                nc.vector.tensor_copy(out=dst, in_=tp[k, half][:].rearrange("p t b -> p b t"))

        def x_quantize(k, half):
            if not ok(k):
                return
            if half == 0:
                xc[k] = const.tile([P, B], U32, name="xc%d" % k, align_bytes=64)
                xs[k] = const.tile([P, B], U8, name="xs%d" % k, align_bytes=64)
            cols = slice(half * BP, (half + 1) * BP)
            nc.vector.quantize_mx(out=xc[k][:, cols].bitcast(FP8X4), scales=xs[k][:, cols], in_=xg[k, half][:])

        def mm1(k, g):
            if not ok(k):
                return
            for t in range(4):
                bank1[k, g, t] = psum.tile([P, B], BANK1, tag="bank", name="bank1")
                cols = slice(t * P, (t + 1) * P)
                nc.tensor.matmul_mx(
                    out=bank1[k, g, t][:],
                    lhsT=w1c[k][:, g, cols].bitcast(FP8X4), lhsT_scale=w1s[k][:, g, cols],
                    rhs=xc[k][:].bitcast(FP8X4), rhs_scale=xs[k][:],
                    start=True, stop=True,
                )

        def relu(k, g):
            if not ok(k):
                return
            rr[k, g] = hp.tile([P, 4, B], F32, tag="rr", name="rr")
            for t in range(4):
                col = (k * G + g) * 4 + t
                nc.scalar.activation(out=rr[k, g][:, t, :], in_=bank1[k, g, t][:], func=ACT.Relu,
                                     bias=b1f[:, col:col + 1], scale=1.0)

        def square(k, g, piece):
            if not ok(k):
                return
            bs = slice(piece * BP, (piece + 1) * BP)
            hg[k, g, piece] = hp.tile([P, 4 * BP], BF16, tag="hg", name="hg", bufs=4, align_bytes=64)
            nc.scalar.activation(out=hg[k, g, piece][:].rearrange("p (c i t) -> p c t i", i=4, t=4),
                                 in_=rr[k, g][:, :, bs].rearrange("p t (c i) -> p c t i", i=4), func=ACT.Square)

        def h_quant(k, g, piece):
            if not ok(k):
                return
            if g == 0:
                hc[k, piece] = hp.tile([P, G, BP], U32, tag="hc", name="hc", bufs=4, align_bytes=64)
                hs[k, piece] = hp.tile([P, G, BP], U8, tag="hs", name="hs", bufs=4, align_bytes=64)
            nc.vector.quantize_mx(out=hc[k, piece][:, g, :].bitcast(FP8X4), scales=hs[k, piece][:, g, :],
                                  in_=hg[k, g, piece][:])

        def mm2(k, piece):
            if not ok(k):
                return
            for bl in range(2):
                ybank[k, piece, bl] = psum.tile([P, D], F32, tag="bank", name="ybank")
                rows_ = slice(bl * P, (bl + 1) * P)
                for g in range(G):
                    nc.tensor.matmul_mx(
                        out=ybank[k, piece, bl][:],
                        lhsT=hc[k, piece][:, g, rows_].bitcast(FP8X4), lhsT_scale=hs[k, piece][:, g, rows_],
                        rhs=w2c[k][:, g, :].bitcast(FP8X4), rhs_scale=w2s[k][:, g, :],
                        start=(g == 0), stop=(g == G - 1),
                    )

        def row_to_all(dst, r):
            nc.tensor.matmul(out=dst, lhsT=ident[:, r:r + 1].to_broadcast([P, P]), rhs=rows[:], start=True, stop=True)

        def spread_b2(k):
            if ok(k) and k % 2 == 0:
                b2ps[k] = psum.tile([P, 2, D], BF16, tag="bank", name="b2ps")
                for u in range(2):
                    row_to_all(b2ps[k][:, u, :], k + u)

        def keep_b2(k):
            if ok(k) and k % 2 == 0:
                b2t[k // 2] = ep.tile([P, 2, D], BF16, tag="b2t", name="b2t", bufs=2)
                nc.scalar.copy(out=b2t[k // 2][:], in_=b2ps[k][:])

        def spread_gamma_beta(k):
            if ok(k):
                gb[k] = psc.tile([P, 2, D], BF16, tag="gb", name="gb")
                for u in range(2):
                    row_to_all(gb[k][:, u, :], (u + 1) * NC + k)

        def ep_a(k, piece):
            if not ok(k):
                return
            ysum[k, piece] = st.tile([P, 2], F32, tag="ysum", name="ysum")
            for bl in range(2):
                yy[k, piece, bl] = ep.tile([P, D], F32, tag="yy", name="yy", bufs=5)
                nc.vector.scalar_tensor_tensor(
                    out=yy[k, piece, bl][:], in0=ybank[k, piece, bl][:], scalar=1.0, in1=b2t[k // 2][:, k % 2, :],
                    op0=ALU.mult, op1=ALU.add, accum_out=ysum[k, piece][:, bl:bl + 1],
                )

        def ep_negmu(k, piece):
            if not ok(k):
                return
            negmu[k, piece] = st.tile([P, 2], F32, tag="negmu", name="negmu")
            nc.gpsimd.tensor_scalar(out=negmu[k, piece][:], in0=ysum[k, piece][:], scalar1=-1.0 / D, scalar2=0.0,
                                    op0=ALU.mult, op1=ALU.add)

        def ep_b(k, piece):
            if not ok(k):
                return
            ssq[k, piece] = st.tile([P, 2], F32, tag="ssq", name="ssq")
            for bl in range(2):
                junk = ep.tile([P, D], BF16, tag="junk", name="junk", bufs=2)
                nc.scalar.activation(out=junk[:], in_=yy[k, piece, bl][:], func=ACT.Square,
                                     bias=negmu[k, piece][:, bl:bl + 1], scale=1.0, accum_out=ssq[k, piece][:, bl:bl + 1])

        def ep_std(k, piece):
            if not ok(k):
                return
            std[k, piece] = st.tile([P, 2], F32, tag="std", name="std")
            nc.gpsimd.tensor_scalar(out=std[k, piece][:], in0=ssq[k, piece][:], scalar1=1.0 / D, scalar2=LN_EPS,
                                    op0=ALU.mult, op1=ALU.add)

        def ep_rstd(k, piece):
            if not ok(k):
                return
            rstd[k, piece] = st.tile([P, 2], F32, tag="rstd", name="rstd")
            nc.gpsimd.tensor_tensor(out=rstd[k, piece][:], in0=std[k, piece][:], in1=mhalf[:], op=ALU.pow)

        def ep_c(k, piece):
            if not ok(k):
                return
            for bl in range(2):
                cg[k, piece, bl] = ep.tile([P, D], F32, tag="cg", name="cg")
                nc.vector.scalar_tensor_tensor(
                    out=cg[k, piece, bl][:], in0=yy[k, piece, bl][:], scalar=negmu[k, piece][:, bl:bl + 1],
                    in1=gb[k][:, 0, :], op0=ALU.add, op1=ALU.mult,
                )

        def ep_d(k, piece):
            if not ok(k):
                return
            for bl in range(2):
                bt = 2 * piece + bl
                res = ep.tile([P, D], F32, tag="res", name="res")
                nc.vector.scalar_tensor_tensor(
                    out=res[:], in0=cg[k, piece, bl][:], scalar=rstd[k, piece][:, bl:bl + 1],
                    in1=gb[k][:, 1, :], op0=ALU.mult, op1=ALU.add,
                )
                nc.sync.dma_start(out=out[bt * P:(bt + 1) * P, k * D:(k + 1) * D], in_=res[:])

        b1raw = const.tile([P, NC * G, 4], BF16, name="b1raw")
        nc.scalar.dma_start(out=b1raw[:], in_=b1.rearrange("k (g p t) -> p (k g) t", g=G, t=4))
        rows = const.tile([P, D], BF16, name="rows")
        nc.gpsimd.memset(rows[:], 0.0)
        nc.scalar.dma_start(out=rows[0:NC, :], in_=b2)
        nc.scalar.dma_start(out=rows[NC:2 * NC, :], in_=gamma)
        nc.scalar.dma_start(out=rows[2 * NC:3 * NC, :], in_=beta)
        ident = const.tile([P, P], BF16, name="ident")
        make_identity(nc, ident[:])
        mhalf = const.tile([P, 2], F32, name="mhalf")
        nc.gpsimd.memset(mhalf[:], -0.5)
        b1f = const.tile([P, NC * G * 4], F32, name="b1f")
        nc.gpsimd.tensor_copy(out=b1f[:], in_=b1raw[:].rearrange("p c t -> p (c t)"))

        tri_sb = []
        for bt in range(BT):
            tri_sb.append(const.tile([P, APC * NC], BF16, name="tri%d" % bt))
            nc.sync.dma_start(out=tri_sb[bt][:], in_=tri[bt * P:(bt + 1) * P, :])
        load_w1(0)
        load_w2(0)
        load_w1(1)
        load_w2(1)

        x_transposes(0, 0)
        x_transposes(0, 1)
        x_copy(0, 0, "S")
        x_transposes(1, 0)
        x_transposes(1, 1)
        x_copy(1, 0, "S")
        x_quantize(0, 0)
        x_transposes(0, 2)
        x_transposes(0, 3)
        x_copy(0, 1, "S")
        x_quantize(1, 0)
        w_interleave(0)
        x_quantize(0, 1)
        w_quantize(0)
        mm1(0, 0)
        w_interleave(1)
        x_transposes(1, 2)
        x_transposes(1, 3)
        w_interleave(2)
        w_quantize(1)
        state["chunk"] = 3

        for i in range(NC + 1):
            kx = i + 2
            ep_a(i - 1, 0)
            relu(i, 0)
            mm1(i, 1)
            spread_b2(i)
            fill()
            ep_negmu(i - 1, 0)
            x_transposes(kx, 0)
            x_transposes(kx, 1)
            ep_a(i - 1, 1)
            if i == 0:
                x_copy(1, 1, "V")
            square(i, 0, 0)
            square(i, 0, 1)
            ep_c(i - 1, 0)
            ep_negmu(i - 1, 1)
            h_quant(i, 0, 0)
            h_quant(i, 0, 1)
            ep_b(i - 1, 0)
            ep_b(i - 1, 1)
            ep_std(i - 1, 0)
            keep_b2(i)
            ep_std(i - 1, 1)
            ep_c(i - 1, 1)
            fill()
            if i == 0:
                x_quantize(1, 1)
            x_copy(kx, 0, "S")
            x_transposes(kx, 2)
            x_transposes(kx, 3)
            relu(i, 1)
            ep_rstd(i - 1, 0)
            ep_rstd(i - 1, 1)
            fill()
            ep_d(i - 1, 0)
            x_quantize(kx, 0)
            mm1(i + 1, 0)
            ep_d(i - 1, 1)
            spread_gamma_beta(i)
            square(i, 1, 0)
            h_quant(i, 1, 0)
            mm2(i, 0)
            x_copy(kx, 1, "S")
            square(i, 1, 1)
            fill()
            x_quantize(kx, 1)
            h_quant(i, 1, 1)
            mm2(i, 1)
